import numpy as np
import ml_dtypes

BF16 = ml_dtypes.bfloat16


def bf(x):
    return np.asarray(x, np.float32).astype(BF16)


def f32(x):
    return np.asarray(x, np.float32)


def f64(x):
    return np.asarray(x).astype(np.float64)


def striped(idx):
    return np.tile(idx.reshape(-1, 16).T, (8, 1))


U, HX, XD, RD, S, N = 128, 256, 128, 128, 2048, 512
STD = 0.1
BASE = 10000.0


def pos_table():
    k = np.arange(S, dtype=np.float32)[None, :]
    i = np.arange(HX // 2, dtype=np.float32)[:, None]
    expo = (2.0 * i / HX).astype(np.float32)
    ang = (k / np.power(np.float32(BASE), expo).astype(np.float32)).astype(np.float32).astype(np.float64)
    p = np.zeros((HX, S))
    p[0::2] = np.sin(ang)
    p[1::2] = np.cos(ang)
    return p


def setup_inputs():
    return {
        "features": bf(np.random.standard_normal((U, S))),
        "pos": f32(pos_table()),
        "w1": bf(np.random.standard_normal((U, HX)) / np.sqrt(U)),
        "b1": f32(0.1 * np.random.standard_normal((HX, 1))),
        "w2": bf(np.random.standard_normal((HX, XD)) / np.sqrt(HX)),
        "b2": f32(0.1 * np.random.standard_normal((XD, 1))),
        "w3x": bf(np.random.standard_normal((XD, RD)) / np.sqrt(XD)),
        "w3y": f32(0.5 * np.random.standard_normal((RD, 1))),
        "b3": f32(0.1 * np.random.standard_normal((RD, 1))),
        "context": f32(np.random.standard_normal((1, N))),
        "noise": f32(np.random.standard_normal((1, N))),
        "offs": striped(np.random.permutation(np.tile(np.arange(S), 2))[:N]),
    }


def reference(features, pos, w1, b1, w2, b2, w3x, w3y, b3, context, noise, offs):
    idx = offs[:16].T.reshape(-1)
    h = np.maximum(f64(w1).T @ f64(features) + f64(b1) + f64(pos), 0.0)
    xhat = f64(w2).T @ h + f64(b2)
    y = f64(context) + STD * f64(noise)
    return np.maximum(f64(w3x).T @ xhat[:, idx] + f64(w3y) * y + f64(b3), 0.0)

@@ -1,0 +1,116 @@
+import concourse.mybir as mybir
+
+BF16, F32, U16 = mybir.dt.bfloat16, mybir.dt.float32, mybir.dt.uint16
+ADD, MULT, MAX = mybir.AluOpType.add, mybir.AluOpType.mult, mybir.AluOpType.max
+RELU, IDENTITY = mybir.ActivationFunctionType.Relu, mybir.ActivationFunctionType.Identity
+
+P = 128
+S = 2048
+N = 512
+BLOCKS = 2
+CHUNK = 512
+CHUNKS = S // CHUNK
+PIECE = 256
+PIECES = N // PIECE
+STD = 0.1
+
+FLOPS = 2 * P * (BLOCKS * P) * S + 2 * (BLOCKS * P) * P * S + 2 * P * P * N
+
+
+def tile_cnp_mlp_mean_kernel(
+    tc, features, pos, w1, b1, w2, b2, w3x, w3y, b3, context, noise, offs, out
+):
+    nc = tc.nc
+    with (
+        tc.tile_pool(name="held", bufs=1) as held,
+        tc.tile_pool(name="work", bufs=4) as work,
+        tc.psum_pool(name="hidden_banks", bufs=4) as hidden_banks,
+        tc.psum_pool(name="encoded_banks", bufs=2) as encoded_banks,
+        tc.psum_pool(name="out_banks", bufs=1) as out_banks,
+    ):
+        offsets = held.tile([P, N // 16], U16, name="offsets")
+        nc.sync.dma_start(offsets[:], offs)
+
+        w1_sb = held.tile([P, BLOCKS * P], BF16, name="w1_sb")
+        nc.sync.dma_start(w1_sb[:], w1)
+        feat = held.tile([P, S], BF16, name="feat")
+        pos_sb = [held.tile([P, S], F32, name=f"pos_sb{k}") for k in range(BLOCKS)]
+        for c in range(CHUNKS):
+            cols = slice(c * CHUNK, (c + 1) * CHUNK)
+            nc.scalar.dma_start(feat[:, cols], features[:, cols])
+            nc.sync.dma_start(pos_sb[0][:, cols], pos[0:P, cols])
+            nc.scalar.dma_start(pos_sb[1][:, cols], pos[P : 2 * P, cols])
+
+        context_row = held.tile([1, N], F32, name="context_row")
+        nc.gpsimd.dma_start(context_row[:], context)
+        noise_row = held.tile([1, N], F32, name="noise_row")
+        nc.gpsimd.dma_start(noise_row[:], noise)
+        w3y_row = held.tile([1, P], F32, name="w3y_row")
+        nc.gpsimd.dma_start(w3y_row[:], w3y.rearrange("m o -> o m"))
+        b1_sb = [held.tile([P, 1], F32, name=f"b1_sb{k}") for k in range(BLOCKS)]
+        for k in range(BLOCKS):
+            nc.gpsimd.dma_start(b1_sb[k][:], b1[k * P : (k + 1) * P, :])
+        w2_sb = held.tile([P, BLOCKS, P], BF16, name="w2_sb")
+        nc.gpsimd.dma_start(w2_sb[:], w2.rearrange("(k p) m -> p k m", p=P))
+        b2_sb = held.tile([P, 1], F32, name="b2_sb")
+        nc.gpsimd.dma_start(b2_sb[:], b2)
+        w3x_sb = held.tile([P, P], BF16, name="w3x_sb")
+        nc.gpsimd.dma_start(w3x_sb[:], w3x)
+        b3_sb = held.tile([P, 1], F32, name="b3_sb")
+        nc.gpsimd.dma_start(b3_sb[:], b3)
+
+        xhat = held.tile([P, S], BF16, name="xhat")
+        hidden = {}
+
+        def first_layer(c):
+            for k in range(BLOCKS):
+                hidden[c, k] = hidden_banks.tile([P, CHUNK], F32, name="hidden")
+                nc.tensor.matmul(
+                    hidden[c, k][:],
+                    w1_sb[:, k * P : (k + 1) * P],
+                    feat[:, c * CHUNK : (c + 1) * CHUNK],
+                    start=True,
+                    stop=True,
+                )
+
+        first_layer(0)
+
+        y_row = held.tile([1, N], F32, name="y_row")
+        nc.vector.scalar_tensor_tensor(
+            y_row[:], noise_row[:], STD, context_row[:], op0=MULT, op1=ADD
+        )
+        out_bank = [out_banks.tile([P, PIECE], F32, name=f"out_bank{i}") for i in range(PIECES)]
+        for i in range(PIECES):
+            nc.tensor.matmul(
+                out_bank[i][:],
+                w3y_row[:],
+                y_row[:, i * PIECE : (i + 1) * PIECE],
+                start=True,
+                stop=False,
+            )
+
+        for c in range(CHUNKS):
+            if c + 1 < CHUNKS:
+                first_layer(c + 1)
+            cols = slice(c * CHUNK, (c + 1) * CHUNK)
+            encoded = encoded_banks.tile([P, CHUNK], F32, name="encoded")
+            for k in range(BLOCKS):
+                summed = work.tile([P, CHUNK], BF16, name="summed")
+                nc.vector.scalar_tensor_tensor(
+                    summed[:], hidden[c, k][:], b1_sb[k][:], pos_sb[k][:, cols], op0=ADD, op1=ADD
+                )
+                h = work.tile([P, CHUNK], BF16, name="h")
+                nc.vector.tensor_scalar_max(h[:], summed[:], 0.0)
+                nc.tensor.matmul(
+                    encoded[:], w2_sb[:, k, :], h[:], start=(k == 0), stop=(k == BLOCKS - 1)
+                )
+            nc.scalar.activation(xhat[:, cols], encoded[:], IDENTITY, bias=b2_sb[:])
+
+        for i in range(PIECES):
+            picked = xhat[:].indirect(offsets[:, i * (PIECE // 16) : (i + 1) * (PIECE // 16)])
+            nc.tensor.matmul(out_bank[i][:], w3x_sb[:], picked, start=False, stop=True)
+        result = [held.tile([P, PIECE], F32, name=f"result{i}") for i in range(PIECES)]
+        nc.scalar.activation(result[0][:], out_bank[0][:], RELU, bias=b3_sb[:])
+        nc.vector.tensor_scalar(result[1][:], out_bank[1][:], b3_sb[:], 0.0, op0=ADD, op1=MAX)
+        nc.scalar.dma_start(out[:, 0:PIECE], result[0][:])
+        nc.sync.dma_start(out[:, PIECE : 2 * PIECE], result[1][:])

@@ -32,31 +32,33 @@ def tile_cnp_mlp_mean_kernel(
         nc.sync.dma_start(offsets[:], offs)
 
         w1_sb = held.tile([P, BLOCKS * P], BF16, name="w1_sb")
-        nc.sync.dma_start(w1_sb[:], w1)
+        b1_sb = [held.tile([P, 1], F32, name=f"b1_sb{k}") for k in range(BLOCKS)]
         feat = held.tile([P, S], BF16, name="feat")
         pos_sb = [held.tile([P, S], F32, name=f"pos_sb{k}") for k in range(BLOCKS)]
+        context_row = held.tile([1, N], F32, name="context_row")
+        noise_row = held.tile([1, N], F32, name="noise_row")
+        w3y_row = held.tile([1, P], F32, name="w3y_row")
+        w2_sb = held.tile([P, BLOCKS, P], BF16, name="w2_sb")
+        b2_sb = held.tile([P, 1], F32, name="b2_sb")
+        w3x_sb = held.tile([P, P], BF16, name="w3x_sb")
+        b3_sb = held.tile([P, 1], F32, name="b3_sb")
+
+        nc.sync.dma_start(w1_sb[:], w1)
+        nc.sync.dma_start(b1_sb[0][:], b1[0:P, :])
+        nc.scalar.dma_start(b1_sb[1][:], b1[P : 2 * P, :])
         for c in range(CHUNKS):
             cols = slice(c * CHUNK, (c + 1) * CHUNK)
             nc.scalar.dma_start(feat[:, cols], features[:, cols])
             nc.sync.dma_start(pos_sb[0][:, cols], pos[0:P, cols])
             nc.scalar.dma_start(pos_sb[1][:, cols], pos[P : 2 * P, cols])
+            if c == 0:
+                nc.sync.dma_start(context_row[:], context)
+                nc.sync.dma_start(noise_row[:], noise)
+                nc.sync.dma_start(w3y_row[:], w3y.rearrange("m o -> o m"))
 
-        context_row = held.tile([1, N], F32, name="context_row")
-        nc.gpsimd.dma_start(context_row[:], context)
-        noise_row = held.tile([1, N], F32, name="noise_row")
-        nc.gpsimd.dma_start(noise_row[:], noise)
-        w3y_row = held.tile([1, P], F32, name="w3y_row")
-        nc.gpsimd.dma_start(w3y_row[:], w3y.rearrange("m o -> o m"))
-        b1_sb = [held.tile([P, 1], F32, name=f"b1_sb{k}") for k in range(BLOCKS)]
-        for k in range(BLOCKS):
-            nc.gpsimd.dma_start(b1_sb[k][:], b1[k * P : (k + 1) * P, :])
-        w2_sb = held.tile([P, BLOCKS, P], BF16, name="w2_sb")
         nc.gpsimd.dma_start(w2_sb[:], w2.rearrange("(k p) m -> p k m", p=P))
-        b2_sb = held.tile([P, 1], F32, name="b2_sb")
         nc.gpsimd.dma_start(b2_sb[:], b2)
-        w3x_sb = held.tile([P, P], BF16, name="w3x_sb")
         nc.gpsimd.dma_start(w3x_sb[:], w3x)
-        b3_sb = held.tile([P, 1], F32, name="b3_sb")
         nc.gpsimd.dma_start(b3_sb[:], b3)
 
         xhat = held.tile([P, S], BF16, name="xhat")

@@ -8,8 +8,10 @@ P = 128
 S = 2048
 N = 512
 BLOCKS = 2
-CHUNK = 512
-CHUNKS = S // CHUNK
+BANK = 512
+WIDTHS = [BANK // 2] + [BANK] * (S // BANK - 1) + [BANK // 2]
+STARTS = [sum(WIDTHS[:c]) for c in range(len(WIDTHS))]
+CHUNKS = len(WIDTHS)
 PIECE = 256
 PIECES = N // PIECE
 STD = 0.1
@@ -23,54 +25,71 @@ def tile_cnp_mlp_mean_kernel(
     nc = tc.nc
     with (
         tc.tile_pool(name="held", bufs=1) as held,
-        tc.tile_pool(name="work", bufs=4) as work,
+        tc.tile_pool(name="work", bufs=BLOCKS * CHUNKS) as work,
         tc.psum_pool(name="hidden_banks", bufs=4) as hidden_banks,
         tc.psum_pool(name="encoded_banks", bufs=2) as encoded_banks,
         tc.psum_pool(name="out_banks", bufs=1) as out_banks,
     ):
         offsets = held.tile([P, N // 16], U16, name="offsets")
-        nc.sync.dma_start(offsets[:], offs)
-
         w1_sb = held.tile([P, BLOCKS * P], BF16, name="w1_sb")
-        b1_sb = [held.tile([P, 1], F32, name=f"b1_sb{k}") for k in range(BLOCKS)]
-        feat = held.tile([P, S], BF16, name="feat")
-        pos_sb = [held.tile([P, S], F32, name=f"pos_sb{k}") for k in range(BLOCKS)]
+        feat_cols = [(0, STARTS[2]), (STARTS[2], S)]
+        feat = [held.tile([P, b - a], BF16, name=f"feat{i}") for i, (a, b) in enumerate(feat_cols)]
+        pos_sb = [held.tile([P, BLOCKS, w], F32, name=f"pos_sb{c}") for c, w in enumerate(WIDTHS)]
         context_row = held.tile([1, N], F32, name="context_row")
         noise_row = held.tile([1, N], F32, name="noise_row")
         w3y_row = held.tile([1, P], F32, name="w3y_row")
         w2_sb = held.tile([P, BLOCKS, P], BF16, name="w2_sb")
-        b2_sb = held.tile([P, 1], F32, name="b2_sb")
         w3x_sb = held.tile([P, P], BF16, name="w3x_sb")
-        b3_sb = held.tile([P, 1], F32, name="b3_sb")
+        b1_row = held.tile([1, BLOCKS * P], F32, name="b1_row")
+        b2_row = held.tile([1, P], F32, name="b2_row")
+        b3_row = held.tile([1, P], F32, name="b3_row")
 
+        pos_blocks = pos.rearrange("(k p) s -> p k s", p=P)
+
+        def load_pos(c):
+            cols = slice(STARTS[c], STARTS[c] + WIDTHS[c])
+            nc.sync.dma_start(pos_sb[c][:], pos_blocks[:, :, cols])
+
+        nc.scalar.dma_start(b1_row[:], b1.rearrange("a o -> o a"))
+        nc.scalar.dma_start(b2_row[:], b2.rearrange("k o -> o k"))
+        nc.scalar.dma_start(b3_row[:], b3.rearrange("m o -> o m"))
+        nc.scalar.dma_start(context_row[:], context)
+        nc.scalar.dma_start(noise_row[:], noise)
+        nc.scalar.dma_start(w3y_row[:], w3y.rearrange("m o -> o m"))
         nc.sync.dma_start(w1_sb[:], w1)
-        nc.sync.dma_start(b1_sb[0][:], b1[0:P, :])
-        nc.scalar.dma_start(b1_sb[1][:], b1[P : 2 * P, :])
-        for c in range(CHUNKS):
-            cols = slice(c * CHUNK, (c + 1) * CHUNK)
-            nc.scalar.dma_start(feat[:, cols], features[:, cols])
-            nc.sync.dma_start(pos_sb[0][:, cols], pos[0:P, cols])
-            nc.scalar.dma_start(pos_sb[1][:, cols], pos[P : 2 * P, cols])
-            if c == 0:
-                nc.sync.dma_start(context_row[:], context)
-                nc.sync.dma_start(noise_row[:], noise)
-                nc.sync.dma_start(w3y_row[:], w3y.rearrange("m o -> o m"))
+        nc.sync.dma_start(feat[0][:], features[:, : STARTS[2]])
+        load_pos(0)
+        load_pos(1)
+        nc.sync.dma_start(w2_sb[:], w2.rearrange("(k p) m -> p k m", p=P))
+        nc.sync.dma_start(feat[1][:], features[:, STARTS[2] :])
+        load_pos(2)
+        load_pos(3)
+        nc.sync.dma_start(offsets[:], offs)
+        nc.sync.dma_start(w3x_sb[:], w3x)
+        load_pos(4)
 
-        nc.gpsimd.dma_start(w2_sb[:], w2.rearrange("(k p) m -> p k m", p=P))
-        nc.gpsimd.dma_start(b2_sb[:], b2)
-        nc.gpsimd.dma_start(w3x_sb[:], w3x)
-        nc.gpsimd.dma_start(b3_sb[:], b3)
+        one = held.tile([1, 1], F32, name="one")
+        nc.vector.memset(one[:], 1.0)
+        bias_bank = encoded_banks.tile([P, BANK], F32, name="bias_bank", tag="encoded")
+        rows = [b1_row[:, 0:P], b1_row[:, P : 2 * P], b2_row[:], b3_row[:]]
+        for i, row in enumerate(rows):
+            nc.tensor.matmul(bias_bank[:, i : i + 1], row, one[:], start=True, stop=True)
+        bias_sb = held.tile([P, 4], F32, name="bias_sb")
+        nc.vector.tensor_copy(bias_sb[:], bias_bank[:, 0:4])
+        b1_sb, b2_sb, b3_sb = bias_sb[:, 0:BLOCKS], bias_sb[:, 2:3], bias_sb[:, 3:4]
 
         xhat = held.tile([P, S], BF16, name="xhat")
         hidden = {}
 
         def first_layer(c):
+            part = 0 if c < 2 else 1
+            first = STARTS[c] - feat_cols[part][0]
             for k in range(BLOCKS):
-                hidden[c, k] = hidden_banks.tile([P, CHUNK], F32, name="hidden")
+                hidden[c, k] = hidden_banks.tile([P, BANK], F32, name="hidden")
                 nc.tensor.matmul(
-                    hidden[c, k][:],
+                    hidden[c, k][:, : WIDTHS[c]],
                     w1_sb[:, k * P : (k + 1) * P],
-                    feat[:, c * CHUNK : (c + 1) * CHUNK],
+                    feat[part][:, first : first + WIDTHS[c]],
                     start=True,
                     stop=True,
                 )
@@ -94,25 +113,38 @@ def tile_cnp_mlp_mean_kernel(
         for c in range(CHUNKS):
             if c + 1 < CHUNKS:
                 first_layer(c + 1)
-            cols = slice(c * CHUNK, (c + 1) * CHUNK)
-            encoded = encoded_banks.tile([P, CHUNK], F32, name="encoded")
+            width = WIDTHS[c]
+            cols = slice(STARTS[c], STARTS[c] + width)
+            encoded = encoded_banks.tile([P, BANK], F32, name="encoded")
             for k in range(BLOCKS):
-                summed = work.tile([P, CHUNK], BF16, name="summed")
+                summed = work.tile([P, BANK], BF16, name="summed")
                 nc.vector.scalar_tensor_tensor(
-                    summed[:], hidden[c, k][:], b1_sb[k][:], pos_sb[k][:, cols], op0=ADD, op1=ADD
+                    summed[:, :width],
+                    hidden[c, k][:, :width],
+                    b1_sb[:, k : k + 1],
+                    pos_sb[c][:, k, :],
+                    op0=ADD,
+                    op1=ADD,
                 )
-                h = work.tile([P, CHUNK], BF16, name="h")
-                nc.vector.tensor_scalar_max(h[:], summed[:], 0.0)
+                h = work.tile([P, BANK], BF16, name="h")
+                if k == 0:
+                    nc.scalar.activation(h[:, :width], summed[:, :width], RELU)
+                else:
+                    nc.vector.tensor_scalar_max(h[:, :width], summed[:, :width], 0.0)
                 nc.tensor.matmul(
-                    encoded[:], w2_sb[:, k, :], h[:], start=(k == 0), stop=(k == BLOCKS - 1)
+                    encoded[:, :width],
+                    w2_sb[:, k, :],
+                    h[:, :width],
+                    start=(k == 0),
+                    stop=(k == BLOCKS - 1),
                 )
-            nc.scalar.activation(xhat[:, cols], encoded[:], IDENTITY, bias=b2_sb[:])
+            nc.scalar.activation(xhat[:, cols], encoded[:, :width], IDENTITY, bias=b2_sb)
 
         for i in range(PIECES):
             picked = xhat[:].indirect(offsets[:, i * (PIECE // 16) : (i + 1) * (PIECE // 16)])
             nc.tensor.matmul(out_bank[i][:], w3x_sb[:], picked, start=False, stop=True)
         result = [held.tile([P, PIECE], F32, name=f"result{i}") for i in range(PIECES)]
-        nc.scalar.activation(result[0][:], out_bank[0][:], RELU, bias=b3_sb[:])
-        nc.vector.tensor_scalar(result[1][:], out_bank[1][:], b3_sb[:], 0.0, op0=ADD, op1=MAX)
+        nc.scalar.activation(result[0][:], out_bank[0][:], RELU, bias=b3_sb)
+        nc.vector.tensor_scalar(result[1][:], out_bank[1][:], b3_sb, 0.0, op0=ADD, op1=MAX)
         nc.scalar.dma_start(out[:, 0:PIECE], result[0][:])
         nc.sync.dma_start(out[:, PIECE : 2 * PIECE], result[1][:])

@@ -1,7 +1,7 @@
 import concourse.mybir as mybir
 
 BF16, F32, U16 = mybir.dt.bfloat16, mybir.dt.float32, mybir.dt.uint16
-ADD, MULT, MAX = mybir.AluOpType.add, mybir.AluOpType.mult, mybir.AluOpType.max
+ADD, MULT = mybir.AluOpType.add, mybir.AluOpType.mult
 RELU, IDENTITY = mybir.ActivationFunctionType.Relu, mybir.ActivationFunctionType.Identity
 
 P = 128
@@ -12,6 +12,8 @@ BANK = 512
 WIDTHS = [BANK // 2] + [BANK] * (S // BANK - 1) + [BANK // 2]
 STARTS = [sum(WIDTHS[:c]) for c in range(len(WIDTHS))]
 CHUNKS = len(WIDTHS)
+AHEAD = 2
+WARMUPS = 3
 PIECE = 256
 PIECES = N // PIECE
 STD = 0.1
@@ -25,126 +27,132 @@ def tile_cnp_mlp_mean_kernel(
     nc = tc.nc
     with (
         tc.tile_pool(name="held", bufs=1) as held,
-        tc.tile_pool(name="work", bufs=BLOCKS * CHUNKS) as work,
-        tc.psum_pool(name="hidden_banks", bufs=4) as hidden_banks,
+        tc.tile_pool(name="work", bufs=CHUNKS) as work,
+        tc.psum_pool(name="hidden_banks", bufs=AHEAD * BLOCKS) as hidden_banks,
         tc.psum_pool(name="encoded_banks", bufs=2) as encoded_banks,
         tc.psum_pool(name="out_banks", bufs=1) as out_banks,
     ):
         offsets = held.tile([P, N // 16], U16, name="offsets")
         w1_sb = held.tile([P, BLOCKS * P], BF16, name="w1_sb")
-        feat_cols = [(0, STARTS[2]), (STARTS[2], S)]
-        feat = [held.tile([P, b - a], BF16, name=f"feat{i}") for i, (a, b) in enumerate(feat_cols)]
-        pos_sb = [held.tile([P, BLOCKS, w], F32, name=f"pos_sb{c}") for c, w in enumerate(WIDTHS)]
+        feat = held.tile([P, S], BF16, name="feat")
+        pos_sb = held.tile([P, BLOCKS, S], F32, name="pos_sb")
         context_row = held.tile([1, N], F32, name="context_row")
         noise_row = held.tile([1, N], F32, name="noise_row")
-        w3y_row = held.tile([1, P], F32, name="w3y_row")
         w2_sb = held.tile([P, BLOCKS, P], BF16, name="w2_sb")
         w3x_sb = held.tile([P, P], BF16, name="w3x_sb")
-        b1_row = held.tile([1, BLOCKS * P], F32, name="b1_row")
+        b1_sb = held.tile([P, BLOCKS], F32, name="b1_sb")
         b2_row = held.tile([1, P], F32, name="b2_row")
-        b3_row = held.tile([1, P], F32, name="b3_row")
+        one = held.tile([1, 1], F32, name="one")
+        zeros = held.tile([P, BANK], BF16, name="zeros")
+        w3y_rows = held.tile([P, P], F32, name="w3y_rows")
+        y_rows = held.tile([P, N], F32, name="y_rows")
+        nc.gpsimd.memset(zeros[:], 0.0)
+        nc.gpsimd.memset(one[:], 1.0)
+        nc.gpsimd.memset(w3y_rows[:], 0.0)
+        nc.gpsimd.memset(y_rows[:], 0.0)
+        nc.gpsimd.memset(y_rows[0:2, :], 1.0)
 
         pos_blocks = pos.rearrange("(k p) s -> p k s", p=P)
 
         def load_pos(c):
             cols = slice(STARTS[c], STARTS[c] + WIDTHS[c])
-            nc.sync.dma_start(pos_sb[c][:], pos_blocks[:, :, cols])
+            nc.sync.dma_start(pos_sb[:, :, cols], pos_blocks[:, :, cols])
 
-        nc.scalar.dma_start(b1_row[:], b1.rearrange("a o -> o a"))
-        nc.scalar.dma_start(b2_row[:], b2.rearrange("k o -> o k"))
-        nc.scalar.dma_start(b3_row[:], b3.rearrange("m o -> o m"))
-        nc.scalar.dma_start(context_row[:], context)
-        nc.scalar.dma_start(noise_row[:], noise)
-        nc.scalar.dma_start(w3y_row[:], w3y.rearrange("m o -> o m"))
         nc.sync.dma_start(w1_sb[:], w1)
-        nc.sync.dma_start(feat[0][:], features[:, : STARTS[2]])
+        nc.sync.dma_start(feat[:, : STARTS[AHEAD]], features[:, : STARTS[AHEAD]])
         load_pos(0)
         load_pos(1)
         nc.sync.dma_start(w2_sb[:], w2.rearrange("(k p) m -> p k m", p=P))
-        nc.sync.dma_start(feat[1][:], features[:, STARTS[2] :])
+        nc.sync.dma_start(feat[:, STARTS[AHEAD] :], features[:, STARTS[AHEAD] :])
         load_pos(2)
         load_pos(3)
         nc.sync.dma_start(offsets[:], offs)
         nc.sync.dma_start(w3x_sb[:], w3x)
         load_pos(4)
+        with nc.allow_non_contiguous_dma(reason="256 biases, one value a partition and block"):
+            nc.scalar.dma_start(b1_sb[:], b1.rearrange("(k p) o -> p (k o)", p=P))
+        nc.scalar.dma_start(b2_row[:], b2.rearrange("k o -> o k"))
+        nc.scalar.dma_start(context_row[:], context)
+        nc.scalar.dma_start(noise_row[:], noise)
+        nc.scalar.dma_start(w3y_rows[0:1, :], w3y.rearrange("m o -> o m"))
+        nc.scalar.dma_start(w3y_rows[1:2, :], b3.rearrange("m o -> o m"))
 
-        one = held.tile([1, 1], F32, name="one")
-        nc.vector.memset(one[:], 1.0)
-        bias_bank = encoded_banks.tile([P, BANK], F32, name="bias_bank", tag="encoded")
-        rows = [b1_row[:, 0:P], b1_row[:, P : 2 * P], b2_row[:], b3_row[:]]
-        for i, row in enumerate(rows):
-            nc.tensor.matmul(bias_bank[:, i : i + 1], row, one[:], start=True, stop=True)
-        bias_sb = held.tile([P, 4], F32, name="bias_sb")
-        nc.vector.tensor_copy(bias_sb[:], bias_bank[:, 0:4])
-        b1_sb, b2_sb, b3_sb = bias_sb[:, 0:BLOCKS], bias_sb[:, 2:3], bias_sb[:, 3:4]
+        warm_bank = hidden_banks.tile([P, BANK], F32, name="warm_bank", tag="hidden")
+        for i in range(WARMUPS):
+            nc.tensor.matmul(warm_bank[:], zeros[:, 0:P], zeros[:], start=True, stop=True)
+
 
         xhat = held.tile([P, S], BF16, name="xhat")
         hidden = {}
+        out_bank = [out_banks.tile([P, PIECE], F32, name=f"out_bank{i}") for i in range(PIECES)]
 
         def first_layer(c):
-            part = 0 if c < 2 else 1
-            first = STARTS[c] - feat_cols[part][0]
             for k in range(BLOCKS):
                 hidden[c, k] = hidden_banks.tile([P, BANK], F32, name="hidden")
                 nc.tensor.matmul(
                     hidden[c, k][:, : WIDTHS[c]],
                     w1_sb[:, k * P : (k + 1) * P],
-                    feat[part][:, first : first + WIDTHS[c]],
+                    feat[:, STARTS[c] : STARTS[c] + WIDTHS[c]],
                     start=True,
                     stop=True,
                 )
 
-        first_layer(0)
-
-        y_row = held.tile([1, N], F32, name="y_row")
-        nc.vector.scalar_tensor_tensor(
-            y_row[:], noise_row[:], STD, context_row[:], op0=MULT, op1=ADD
-        )
-        out_bank = [out_banks.tile([P, PIECE], F32, name=f"out_bank{i}") for i in range(PIECES)]
-        for i in range(PIECES):
-            nc.tensor.matmul(
-                out_bank[i][:],
-                w3y_row[:],
-                y_row[:, i * PIECE : (i + 1) * PIECE],
-                start=True,
-                stop=False,
+        def observed_term():
+            nc.vector.scalar_tensor_tensor(
+                y_rows[0:1, :], noise_row[:], STD, context_row[:], op0=MULT, op1=ADD
             )
+            for i in range(PIECES):
+                nc.tensor.matmul(
+                    out_bank[i][:],
+                    w3y_rows[:],
+                    y_rows[:, i * PIECE : (i + 1) * PIECE],
+                    start=True,
+                    stop=False,
+                )
+
+        for c in range(AHEAD):
+            first_layer(c)
+
+        b2_bank = encoded_banks.tile([P, BANK], F32, name="b2_bank", tag="encoded")
+        nc.tensor.matmul(b2_bank[:, 0:1], b2_row[:], one[:], start=True, stop=True)
+        b2_sb = held.tile([P, 1], F32, name="b2_sb")
+        nc.scalar.copy(b2_sb[:], b2_bank[:, 0:1])
 
         for c in range(CHUNKS):
-            if c + 1 < CHUNKS:
-                first_layer(c + 1)
             width = WIDTHS[c]
             cols = slice(STARTS[c], STARTS[c] + width)
-            encoded = encoded_banks.tile([P, BANK], F32, name="encoded")
+            summed = work.tile([P, BLOCKS, width], BF16, name="summed")
             for k in range(BLOCKS):
-                summed = work.tile([P, BANK], BF16, name="summed")
                 nc.vector.scalar_tensor_tensor(
-                    summed[:, :width],
+                    summed[:, k, :],
                     hidden[c, k][:, :width],
                     b1_sb[:, k : k + 1],
-                    pos_sb[c][:, k, :],
+                    pos_sb[:, k, cols],
                     op0=ADD,
                     op1=ADD,
                 )
-                h = work.tile([P, BANK], BF16, name="h")
-                if k == 0:
-                    nc.scalar.activation(h[:, :width], summed[:, :width], RELU)
-                else:
-                    nc.vector.tensor_scalar_max(h[:, :width], summed[:, :width], 0.0)
+            h = work.tile([P, BLOCKS, width], BF16, name="h")
+            nc.vector.tensor_scalar_max(h[:], summed[:], 0.0)
+            if c + AHEAD < CHUNKS:
+                first_layer(c + AHEAD)
+            encoded = encoded_banks.tile([P, BANK], F32, name="encoded")
+            for k in range(BLOCKS):
                 nc.tensor.matmul(
                     encoded[:, :width],
                     w2_sb[:, k, :],
-                    h[:, :width],
+                    h[:, k, :],
                     start=(k == 0),
                     stop=(k == BLOCKS - 1),
                 )
-            nc.scalar.activation(xhat[:, cols], encoded[:, :width], IDENTITY, bias=b2_sb)
+            nc.scalar.activation(xhat[:, cols], encoded[:, :width], IDENTITY, bias=b2_sb[:])
+
+        observed_term()
 
         for i in range(PIECES):
             picked = xhat[:].indirect(offsets[:, i * (PIECE // 16) : (i + 1) * (PIECE // 16)])
             nc.tensor.matmul(out_bank[i][:], w3x_sb[:], picked, start=False, stop=True)
         result = [held.tile([P, PIECE], F32, name=f"result{i}") for i in range(PIECES)]
-        nc.scalar.activation(result[0][:], out_bank[0][:], RELU, bias=b3_sb)
-        nc.vector.tensor_scalar(result[1][:], out_bank[1][:], b3_sb, 0.0, op0=ADD, op1=MAX)
+        nc.scalar.activation(result[0][:], out_bank[0][:], RELU)
+        nc.vector.tensor_scalar_max(result[1][:], out_bank[1][:], 0.0)
         nc.scalar.dma_start(out[:, 0:PIECE], result[0][:])
         nc.sync.dma_start(out[:, PIECE : 2 * PIECE], result[1][:])

@@ -1,7 +1,8 @@
 import concourse.mybir as mybir
+from concourse.masks import make_identity
 
 BF16, F32, U16 = mybir.dt.bfloat16, mybir.dt.float32, mybir.dt.uint16
-ADD, MULT = mybir.AluOpType.add, mybir.AluOpType.mult
+ADD = mybir.AluOpType.add
 RELU, IDENTITY = mybir.ActivationFunctionType.Relu, mybir.ActivationFunctionType.Identity
 
 P = 128
@@ -12,13 +13,17 @@ BANK = 512
 WIDTHS = [BANK // 2] + [BANK] * (S // BANK - 1) + [BANK // 2]
 STARTS = [sum(WIDTHS[:c]) for c in range(len(WIDTHS))]
 CHUNKS = len(WIDTHS)
-AHEAD = 2
+AHEAD = 3
 WARMUPS = 3
 PIECE = 256
 PIECES = N // PIECE
 STD = 0.1
 
 FLOPS = 2 * P * (BLOCKS * P) * S + 2 * (BLOCKS * P) * P * S + 2 * P * P * N
+
+
+def by_tensor(c, k):
+    return k == BLOCKS - 1 and c == CHUNKS - 2
 
 
 def tile_cnp_mlp_mean_kernel(
@@ -30,40 +35,48 @@ def tile_cnp_mlp_mean_kernel(
         tc.tile_pool(name="work", bufs=CHUNKS) as work,
         tc.psum_pool(name="hidden_banks", bufs=AHEAD * BLOCKS) as hidden_banks,
         tc.psum_pool(name="encoded_banks", bufs=2) as encoded_banks,
-        tc.psum_pool(name="out_banks", bufs=1) as out_banks,
     ):
         offsets = held.tile([P, N // 16], U16, name="offsets")
         w1_sb = held.tile([P, BLOCKS * P], BF16, name="w1_sb")
         feat = held.tile([P, S], BF16, name="feat")
         pos_sb = held.tile([P, BLOCKS, S], F32, name="pos_sb")
-        context_row = held.tile([1, N], F32, name="context_row")
-        noise_row = held.tile([1, N], F32, name="noise_row")
         w2_sb = held.tile([P, BLOCKS, P], BF16, name="w2_sb")
         w3x_sb = held.tile([P, P], BF16, name="w3x_sb")
         b1_sb = held.tile([P, BLOCKS], F32, name="b1_sb")
         b2_row = held.tile([1, P], F32, name="b2_row")
         one = held.tile([1, 1], F32, name="one")
         zeros = held.tile([P, BANK], BF16, name="zeros")
+        w3y_pair = held.tile([2, P], F32, name="w3y_pair")
+        pair_scale = held.tile([2, 1], F32, name="pair_scale")
         w3y_rows = held.tile([P, P], F32, name="w3y_rows")
         y_rows = held.tile([P, N], F32, name="y_rows")
+        identity = held.tile([P, P], F32, name="identity")
         nc.gpsimd.memset(zeros[:], 0.0)
+        make_identity(nc, identity[:])
         nc.gpsimd.memset(one[:], 1.0)
+        nc.gpsimd.memset(pair_scale[:], STD)
+        nc.gpsimd.memset(pair_scale[0:1, :], 1.0)
         nc.gpsimd.memset(w3y_rows[:], 0.0)
         nc.gpsimd.memset(y_rows[:], 0.0)
-        nc.gpsimd.memset(y_rows[0:2, :], 1.0)
+        nc.gpsimd.memset(y_rows[0:3, :], 1.0)
 
         pos_blocks = pos.rearrange("(k p) s -> p k s", p=P)
 
         def load_pos(c):
             cols = slice(STARTS[c], STARTS[c] + WIDTHS[c])
-            nc.sync.dma_start(pos_sb[:, :, cols], pos_blocks[:, :, cols])
+            early = [k for k in range(BLOCKS) if by_tensor(c, k)]
+            if early:
+                for k in early + [k for k in range(BLOCKS) if k not in early]:
+                    nc.sync.dma_start(pos_sb[:, k, cols], pos_blocks[:, k, cols])
+            else:
+                nc.sync.dma_start(pos_sb[:, :, cols], pos_blocks[:, :, cols])
 
         nc.sync.dma_start(w1_sb[:], w1)
-        nc.sync.dma_start(feat[:, : STARTS[AHEAD]], features[:, : STARTS[AHEAD]])
+        nc.sync.dma_start(feat[:, : STARTS[2]], features[:, : STARTS[2]])
         load_pos(0)
         load_pos(1)
         nc.sync.dma_start(w2_sb[:], w2.rearrange("(k p) m -> p k m", p=P))
-        nc.sync.dma_start(feat[:, STARTS[AHEAD] :], features[:, STARTS[AHEAD] :])
+        nc.sync.dma_start(feat[:, STARTS[2] :], features[:, STARTS[2] :])
         load_pos(2)
         load_pos(3)
         nc.sync.dma_start(offsets[:], offs)
@@ -72,10 +85,10 @@ def tile_cnp_mlp_mean_kernel(
         with nc.allow_non_contiguous_dma(reason="256 biases, one value a partition and block"):
             nc.scalar.dma_start(b1_sb[:], b1.rearrange("(k p) o -> p (k o)", p=P))
         nc.scalar.dma_start(b2_row[:], b2.rearrange("k o -> o k"))
-        nc.scalar.dma_start(context_row[:], context)
-        nc.scalar.dma_start(noise_row[:], noise)
-        nc.scalar.dma_start(w3y_rows[0:1, :], w3y.rearrange("m o -> o m"))
-        nc.scalar.dma_start(w3y_rows[1:2, :], b3.rearrange("m o -> o m"))
+        nc.scalar.dma_start(y_rows[0:1, :], context)
+        nc.scalar.dma_start(y_rows[1:2, :], noise)
+        nc.scalar.dma_start(w3y_pair[:], w3y.rearrange("m o -> (m o)").partition_broadcast(2))
+        nc.scalar.dma_start(w3y_rows[2:3, :], b3.rearrange("m o -> o m"))
 
         warm_bank = hidden_banks.tile([P, BANK], F32, name="warm_bank", tag="hidden")
         for i in range(WARMUPS):
@@ -84,7 +97,7 @@ def tile_cnp_mlp_mean_kernel(
 
         xhat = held.tile([P, S], BF16, name="xhat")
         hidden = {}
-        out_bank = [out_banks.tile([P, PIECE], F32, name=f"out_bank{i}") for i in range(PIECES)]
+        out_bank = []
 
         def first_layer(c):
             for k in range(BLOCKS):
@@ -94,16 +107,15 @@ def tile_cnp_mlp_mean_kernel(
                     w1_sb[:, k * P : (k + 1) * P],
                     feat[:, STARTS[c] : STARTS[c] + WIDTHS[c]],
                     start=True,
-                    stop=True,
+                    stop=not by_tensor(c, k),
                 )
 
         def observed_term():
-            nc.vector.scalar_tensor_tensor(
-                y_rows[0:1, :], noise_row[:], STD, context_row[:], op0=MULT, op1=ADD
-            )
+            nc.scalar.activation(w3y_rows[0:2, :], w3y_pair[:], IDENTITY, scale=pair_scale[:])
             for i in range(PIECES):
+                out_bank.append(hidden_banks.tile([P, BANK], F32, name=f"out_bank{i}", tag="hidden"))
                 nc.tensor.matmul(
-                    out_bank[i][:],
+                    out_bank[i][:, :PIECE],
                     w3y_rows[:],
                     y_rows[:, i * PIECE : (i + 1) * PIECE],
                     start=True,
@@ -118,21 +130,40 @@ def tile_cnp_mlp_mean_kernel(
         b2_sb = held.tile([P, 1], F32, name="b2_sb")
         nc.scalar.copy(b2_sb[:], b2_bank[:, 0:1])
 
-        for c in range(CHUNKS):
+        h = {c: work.tile([P, BLOCKS, WIDTHS[c]], BF16, name="h") for c in range(CHUNKS)}
+
+        def activate_by_vector(c, blocks):
             width = WIDTHS[c]
-            cols = slice(STARTS[c], STARTS[c] + width)
-            summed = work.tile([P, BLOCKS, width], BF16, name="summed")
-            for k in range(BLOCKS):
+            summed = work.tile([P, blocks, width], BF16, name="summed")
+            for k in range(blocks):
                 nc.vector.scalar_tensor_tensor(
                     summed[:, k, :],
                     hidden[c, k][:, :width],
                     b1_sb[:, k : k + 1],
-                    pos_sb[:, k, cols],
+                    pos_sb[:, k, STARTS[c] : STARTS[c] + width],
                     op0=ADD,
                     op1=ADD,
                 )
-            h = work.tile([P, BLOCKS, width], BF16, name="h")
-            nc.vector.tensor_scalar_max(h[:], summed[:], 0.0)
+            nc.vector.tensor_scalar_max(h[c][:, :blocks, :], summed[:], 0.0)
+
+        def activate_by_tensor(c, k):
+            width = WIDTHS[c]
+            nc.tensor.matmul(
+                hidden[c, k][:, :width],
+                identity[:],
+                pos_sb[:, k, STARTS[c] : STARTS[c] + width],
+                start=False,
+                stop=True,
+            )
+            nc.scalar.activation(h[c][:, k, :], hidden[c, k][:, :width], RELU, bias=b1_sb[:, k : k + 1])
+
+        for c in range(CHUNKS):
+            width = WIDTHS[c]
+            cols = slice(STARTS[c], STARTS[c] + width)
+            activate_by_vector(c, len([k for k in range(BLOCKS) if not by_tensor(c, k)]))
+            for k in range(BLOCKS):
+                if c + 1 < CHUNKS and by_tensor(c + 1, k):
+                    activate_by_tensor(c + 1, k)
             if c + AHEAD < CHUNKS:
                 first_layer(c + AHEAD)
             encoded = encoded_banks.tile([P, BANK], F32, name="encoded")
@@ -140,19 +171,22 @@ def tile_cnp_mlp_mean_kernel(
                 nc.tensor.matmul(
                     encoded[:, :width],
                     w2_sb[:, k, :],
-                    h[:, k, :],
+                    h[c][:, k, :],
                     start=(k == 0),
                     stop=(k == BLOCKS - 1),
                 )
-            nc.scalar.activation(xhat[:, cols], encoded[:, :width], IDENTITY, bias=b2_sb[:])
+            if c < CHUNKS - 1:
+                nc.scalar.activation(xhat[:, cols], encoded[:, :width], IDENTITY, bias=b2_sb[:])
+            else:
+                nc.vector.tensor_scalar_add(xhat[:, cols], encoded[:, :width], b2_sb[:])
 
         observed_term()
 
         for i in range(PIECES):
             picked = xhat[:].indirect(offsets[:, i * (PIECE // 16) : (i + 1) * (PIECE // 16)])
-            nc.tensor.matmul(out_bank[i][:], w3x_sb[:], picked, start=False, stop=True)
+            nc.tensor.matmul(out_bank[i][:, :PIECE], w3x_sb[:], picked, start=False, stop=True)
         result = [held.tile([P, PIECE], F32, name=f"result{i}") for i in range(PIECES)]
-        nc.scalar.activation(result[0][:], out_bank[0][:], RELU)
-        nc.vector.tensor_scalar_max(result[1][:], out_bank[1][:], 0.0)
+        nc.scalar.activation(result[0][:], out_bank[0][:, :PIECE], RELU)
+        nc.vector.tensor_scalar_max(result[1][:], out_bank[1][:, :PIECE], 0.0)
         nc.scalar.dma_start(out[:, 0:PIECE], result[0][:])
         nc.sync.dma_start(out[:, PIECE : 2 * PIECE], result[1][:])

@@ -72,11 +72,10 @@ def tile_cnp_mlp_mean_kernel(
                 nc.sync.dma_start(pos_sb[:, :, cols], pos_blocks[:, :, cols])
 
         nc.sync.dma_start(w1_sb[:], w1)
-        nc.sync.dma_start(feat[:, : STARTS[2]], features[:, : STARTS[2]])
+        nc.sync.dma_start(feat[:], features)
         load_pos(0)
         load_pos(1)
         nc.sync.dma_start(w2_sb[:], w2.rearrange("(k p) m -> p k m", p=P))
-        nc.sync.dma_start(feat[:, STARTS[2] :], features[:, STARTS[2] :])
         load_pos(2)
         load_pos(3)
         nc.sync.dma_start(offsets[:], offs)

@@ -13,7 +13,7 @@ BANK = 512
 WIDTHS = [BANK // 2] + [BANK] * (S // BANK - 1) + [BANK // 2]
 STARTS = [sum(WIDTHS[:c]) for c in range(len(WIDTHS))]
 CHUNKS = len(WIDTHS)
-AHEAD = 3
+AHEAD = 2
 WARMUPS = 3
 PIECE = 256
 PIECES = N // PIECE
@@ -35,6 +35,7 @@ def tile_cnp_mlp_mean_kernel(
         tc.tile_pool(name="work", bufs=CHUNKS) as work,
         tc.psum_pool(name="hidden_banks", bufs=AHEAD * BLOCKS) as hidden_banks,
         tc.psum_pool(name="encoded_banks", bufs=2) as encoded_banks,
+        tc.psum_pool(name="out_banks", bufs=1) as out_banks,
     ):
         offsets = held.tile([P, N // 16], U16, name="offsets")
         w1_sb = held.tile([P, BLOCKS * P], BF16, name="w1_sb")
@@ -99,10 +100,14 @@ def tile_cnp_mlp_mean_kernel(
         out_bank = []
 
         def first_layer(c):
+            width = WIDTHS[c]
+            blocks_a_bank = BANK // width
             for k in range(BLOCKS):
-                hidden[c, k] = hidden_banks.tile([P, BANK], F32, name="hidden")
+                if k % blocks_a_bank == 0:
+                    bank = hidden_banks.tile([P, BANK], F32, name="hidden")
+                hidden[c, k] = bank[:, (k % blocks_a_bank) * width : (k % blocks_a_bank + 1) * width]
                 nc.tensor.matmul(
-                    hidden[c, k][:, : WIDTHS[c]],
+                    hidden[c, k],
                     w1_sb[:, k * P : (k + 1) * P],
                     feat[:, STARTS[c] : STARTS[c] + WIDTHS[c]],
                     start=True,
@@ -112,7 +117,7 @@ def tile_cnp_mlp_mean_kernel(
         def observed_term():
             nc.scalar.activation(w3y_rows[0:2, :], w3y_pair[:], IDENTITY, scale=pair_scale[:])
             for i in range(PIECES):
-                out_bank.append(hidden_banks.tile([P, BANK], F32, name=f"out_bank{i}", tag="hidden"))
+                out_bank.append(out_banks.tile([P, BANK], F32, name=f"out_bank{i}"))
                 nc.tensor.matmul(
                     out_bank[i][:, :PIECE],
                     w3y_rows[:],
@@ -123,6 +128,8 @@ def tile_cnp_mlp_mean_kernel(
 
         for c in range(AHEAD):
             first_layer(c)
+
+        observed_term()
 
         b2_bank = encoded_banks.tile([P, BANK], F32, name="b2_bank", tag="encoded")
         nc.tensor.matmul(b2_bank[:, 0:1], b2_row[:], one[:], start=True, stop=True)
@@ -137,7 +144,7 @@ def tile_cnp_mlp_mean_kernel(
             for k in range(blocks):
                 nc.vector.scalar_tensor_tensor(
                     summed[:, k, :],
-                    hidden[c, k][:, :width],
+                    hidden[c, k],
                     b1_sb[:, k : k + 1],
                     pos_sb[:, k, STARTS[c] : STARTS[c] + width],
                     op0=ADD,
@@ -148,23 +155,23 @@ def tile_cnp_mlp_mean_kernel(
         def activate_by_tensor(c, k):
             width = WIDTHS[c]
             nc.tensor.matmul(
-                hidden[c, k][:, :width],
+                hidden[c, k],
                 identity[:],
                 pos_sb[:, k, STARTS[c] : STARTS[c] + width],
                 start=False,
                 stop=True,
             )
-            nc.scalar.activation(h[c][:, k, :], hidden[c, k][:, :width], RELU, bias=b1_sb[:, k : k + 1])
+            nc.scalar.activation(h[c][:, k, :], hidden[c, k], RELU, bias=b1_sb[:, k : k + 1])
 
         for c in range(CHUNKS):
             width = WIDTHS[c]
             cols = slice(STARTS[c], STARTS[c] + width)
             activate_by_vector(c, len([k for k in range(BLOCKS) if not by_tensor(c, k)]))
+            if c + AHEAD < CHUNKS:
+                first_layer(c + AHEAD)
             for k in range(BLOCKS):
                 if c + 1 < CHUNKS and by_tensor(c + 1, k):
                     activate_by_tensor(c + 1, k)
-            if c + AHEAD < CHUNKS:
-                first_layer(c + AHEAD)
             encoded = encoded_banks.tile([P, BANK], F32, name="encoded")
             for k in range(BLOCKS):
                 nc.tensor.matmul(
@@ -178,8 +185,6 @@ def tile_cnp_mlp_mean_kernel(
                 nc.scalar.activation(xhat[:, cols], encoded[:, :width], IDENTITY, bias=b2_sb[:])
             else:
                 nc.vector.tensor_scalar_add(xhat[:, cols], encoded[:, :width], b2_sb[:])
-
-        observed_term()
 
         for i in range(PIECES):
             picked = xhat[:].indirect(offsets[:, i * (PIECE // 16) : (i + 1) * (PIECE // 16)])

import concourse.mybir as mybir
from concourse.masks import make_identity

BF16, F32, U16 = mybir.dt.bfloat16, mybir.dt.float32, mybir.dt.uint16
ADD = mybir.AluOpType.add
RELU, IDENTITY = mybir.ActivationFunctionType.Relu, mybir.ActivationFunctionType.Identity

P = 128
S = 2048
N = 512
BLOCKS = 2
BANK = 512
WIDTHS = [BANK // 2] + [BANK] * (S // BANK - 1) + [BANK // 2]
STARTS = [sum(WIDTHS[:c]) for c in range(len(WIDTHS))]
CHUNKS = len(WIDTHS)
AHEAD = 2
WARMUPS = 3
PIECE = 256
PIECES = N // PIECE
STD = 0.1

FLOPS = 2 * P * (BLOCKS * P) * S + 2 * (BLOCKS * P) * P * S + 2 * P * P * N


def by_tensor(c, k):
    return k == BLOCKS - 1 and c == CHUNKS - 2


def tile_cnp_mlp_mean_kernel(
    tc, features, pos, w1, b1, w2, b2, w3x, w3y, b3, context, noise, offs, out
):
    nc = tc.nc
    with (
        tc.tile_pool(name="held", bufs=1) as held,
        tc.tile_pool(name="work", bufs=CHUNKS) as work,
        tc.psum_pool(name="hidden_banks", bufs=AHEAD * BLOCKS) as hidden_banks,
        tc.psum_pool(name="encoded_banks", bufs=2) as encoded_banks,
        tc.psum_pool(name="out_banks", bufs=1) as out_banks,
    ):
        offsets = held.tile([P, N // 16], U16, name="offsets")
        w1_sb = held.tile([P, BLOCKS * P], BF16, name="w1_sb")
        feat = held.tile([P, S], BF16, name="feat")
        pos_sb = held.tile([P, BLOCKS, S], F32, name="pos_sb")
        w2_sb = held.tile([P, BLOCKS, P], BF16, name="w2_sb")
        w3x_sb = held.tile([P, P], BF16, name="w3x_sb")
        b1_sb = held.tile([P, BLOCKS], F32, name="b1_sb")
        b2_row = held.tile([1, P], F32, name="b2_row")
        one = held.tile([1, 1], F32, name="one")
        zeros = held.tile([P, BANK], BF16, name="zeros")
        w3y_pair = held.tile([2, P], F32, name="w3y_pair")
        pair_scale = held.tile([2, 1], F32, name="pair_scale")
        w3y_rows = held.tile([P, P], F32, name="w3y_rows")
        y_rows = held.tile([P, N], F32, name="y_rows")
        identity = held.tile([P, P], F32, name="identity")
        nc.gpsimd.memset(zeros[:], 0.0)
        make_identity(nc, identity[:])
        nc.gpsimd.memset(one[:], 1.0)
        nc.gpsimd.memset(pair_scale[:], STD)
        nc.gpsimd.memset(pair_scale[0:1, :], 1.0)
        nc.gpsimd.memset(w3y_rows[:], 0.0)
        nc.gpsimd.memset(y_rows[:], 0.0)
        nc.gpsimd.memset(y_rows[0:3, :], 1.0)

        pos_blocks = pos.rearrange("(k p) s -> p k s", p=P)

        def load_pos(c):
            cols = slice(STARTS[c], STARTS[c] + WIDTHS[c])
            early = [k for k in range(BLOCKS) if by_tensor(c, k)]
            if early:
                for k in early + [k for k in range(BLOCKS) if k not in early]:
                    nc.sync.dma_start(pos_sb[:, k, cols], pos_blocks[:, k, cols])
            else:
                nc.sync.dma_start(pos_sb[:, :, cols], pos_blocks[:, :, cols])

        nc.sync.dma_start(w1_sb[:], w1)
        nc.sync.dma_start(feat[:], features)
        load_pos(0)
        load_pos(1)
        nc.sync.dma_start(w2_sb[:], w2.rearrange("(k p) m -> p k m", p=P))
        load_pos(2)
        load_pos(3)
        nc.sync.dma_start(offsets[:], offs)
        nc.sync.dma_start(w3x_sb[:], w3x)
        load_pos(4)
        with nc.allow_non_contiguous_dma(reason="256 biases, one value a partition and block"):
            nc.scalar.dma_start(b1_sb[:], b1.rearrange("(k p) o -> p (k o)", p=P))
        nc.scalar.dma_start(b2_row[:], b2.rearrange("k o -> o k"))
        nc.scalar.dma_start(y_rows[0:1, :], context)
        nc.scalar.dma_start(y_rows[1:2, :], noise)
        nc.scalar.dma_start(w3y_pair[:], w3y.rearrange("m o -> (m o)").partition_broadcast(2))
        nc.scalar.dma_start(w3y_rows[2:3, :], b3.rearrange("m o -> o m"))

        warm_bank = hidden_banks.tile([P, BANK], F32, name="warm_bank", tag="hidden")
        for i in range(WARMUPS):
            nc.tensor.matmul(warm_bank[:], zeros[:, 0:P], zeros[:], start=True, stop=True)


        xhat = held.tile([P, S], BF16, name="xhat")
        hidden = {}
        out_bank = []

        def first_layer(c):
            width = WIDTHS[c]
            blocks_a_bank = BANK // width
            for k in range(BLOCKS):
                if k % blocks_a_bank == 0:
                    bank = hidden_banks.tile([P, BANK], F32, name="hidden")
                hidden[c, k] = bank[:, (k % blocks_a_bank) * width : (k % blocks_a_bank + 1) * width]
                nc.tensor.matmul(
                    hidden[c, k],
                    w1_sb[:, k * P : (k + 1) * P],
                    feat[:, STARTS[c] : STARTS[c] + WIDTHS[c]],
                    start=True,
                    stop=not by_tensor(c, k),
                )

        def observed_term():
            nc.scalar.activation(w3y_rows[0:2, :], w3y_pair[:], IDENTITY, scale=pair_scale[:])
            for i in range(PIECES):
                out_bank.append(out_banks.tile([P, BANK], F32, name=f"out_bank{i}"))
                nc.tensor.matmul(
                    out_bank[i][:, :PIECE],
                    w3y_rows[:],
                    y_rows[:, i * PIECE : (i + 1) * PIECE],
                    start=True,
                    stop=False,
                )

        for c in range(AHEAD):
            first_layer(c)

        observed_term()

        b2_bank = encoded_banks.tile([P, BANK], F32, name="b2_bank", tag="encoded")
        nc.tensor.matmul(b2_bank[:, 0:1], b2_row[:], one[:], start=True, stop=True)
        b2_sb = held.tile([P, 1], F32, name="b2_sb")
        nc.scalar.copy(b2_sb[:], b2_bank[:, 0:1])

        h = {c: work.tile([P, BLOCKS, WIDTHS[c]], BF16, name="h") for c in range(CHUNKS)}

        def activate_by_vector(c, blocks):
            width = WIDTHS[c]
            summed = work.tile([P, blocks, width], BF16, name="summed")
            for k in range(blocks):
                nc.vector.scalar_tensor_tensor(
                    summed[:, k, :],
                    hidden[c, k],
                    b1_sb[:, k : k + 1],
                    pos_sb[:, k, STARTS[c] : STARTS[c] + width],
                    op0=ADD,
                    op1=ADD,
                )
            nc.vector.tensor_scalar_max(h[c][:, :blocks, :], summed[:], 0.0)

        def activate_by_tensor(c, k):
            width = WIDTHS[c]
            nc.tensor.matmul(
                hidden[c, k],
                identity[:],
                pos_sb[:, k, STARTS[c] : STARTS[c] + width],
                start=False,
                stop=True,
            )
            nc.scalar.activation(h[c][:, k, :], hidden[c, k], RELU, bias=b1_sb[:, k : k + 1])

        for c in range(CHUNKS):
            width = WIDTHS[c]
            cols = slice(STARTS[c], STARTS[c] + width)
            activate_by_vector(c, len([k for k in range(BLOCKS) if not by_tensor(c, k)]))
            if c + AHEAD < CHUNKS:
                first_layer(c + AHEAD)
            for k in range(BLOCKS):
                if c + 1 < CHUNKS and by_tensor(c + 1, k):
                    activate_by_tensor(c + 1, k)
            encoded = encoded_banks.tile([P, BANK], F32, name="encoded")
            for k in range(BLOCKS):
                nc.tensor.matmul(
                    encoded[:, :width],
                    w2_sb[:, k, :],
                    h[c][:, k, :],
                    start=(k == 0),
                    stop=(k == BLOCKS - 1),
                )
            if c < CHUNKS - 1:
                nc.scalar.activation(xhat[:, cols], encoded[:, :width], IDENTITY, bias=b2_sb[:])
            else:
                nc.vector.tensor_scalar_add(xhat[:, cols], encoded[:, :width], b2_sb[:])

        for i in range(PIECES):
            picked = xhat[:].indirect(offsets[:, i * (PIECE // 16) : (i + 1) * (PIECE // 16)])
            nc.tensor.matmul(out_bank[i][:, :PIECE], w3x_sb[:], picked, start=False, stop=True)
        result = [held.tile([P, PIECE], F32, name=f"result{i}") for i in range(PIECES)]
        nc.scalar.activation(result[0][:], out_bank[0][:, :PIECE], RELU)
        nc.vector.tensor_scalar_max(result[1][:], out_bank[1][:, :PIECE], 0.0)
        nc.scalar.dma_start(out[:, 0:PIECE], result[0][:])
        nc.sync.dma_start(out[:, PIECE : 2 * PIECE], result[1][:])
